import numpy as np
import ml_dtypes


def mxq(x, axis, fmt="e4m3"):
    dtype, down = {"e4m3": (ml_dtypes.float8_e4m3fn, 7), "e5m2": (ml_dtypes.float8_e5m2, 14)}[fmt]
    v = np.moveaxis(np.asarray(x, np.float32).astype(ml_dtypes.bfloat16).astype(np.float64), axis, -1)
    blocks = v.reshape(v.shape[:-1] + (-1, 32))
    amax = np.abs(blocks).max(-1, keepdims=True)
    byte = np.maximum(np.where(amax > 0, np.frexp(amax)[1] - 1 + 127, 0) - down, 1)
    scale = np.exp2(byte - 127.0)
    codes = (blocks / scale).astype(np.float32).astype(dtype).astype(np.float64)
    return np.moveaxis((codes * scale).reshape(v.shape), -1, axis)


WIDE = False


def mx_kscale(k):
    if not WIDE:
        return np.ones(k)
    levels = np.array([10, -10, 5, -5, 0])
    a = np.random.permutation(np.resize(levels, k // 512 * 4)).reshape(k // 512, 4)
    idx = np.arange(k)
    return np.exp2(a[idx // 512, idx % 128 // 32])


BF16 = ml_dtypes.bfloat16


def bf(x):
    return np.asarray(x, np.float32).astype(BF16)


def f64(x):
    return np.asarray(x).astype(np.float64)


B, P, H, D = 2, 4096, 512, 512


def _length_weights(batch, seqlen):
    lens = np.random.randint(seqlen // 2, seqlen + 1, size=batch)
    tail = 0.25 + 0.5 * np.random.random_sample((batch, seqlen))
    return np.where(np.arange(seqlen)[None, :] < lens[:, None], 1.0, tail)


def setup_inputs():
    s = mx_kscale(D)
    return {"premise_batch": bf(np.random.standard_normal((B, P, D)) * 2.0 * s),
            "premise_mask": bf(_length_weights(B, P)),
            "hypothesis_batch": bf(np.random.standard_normal((B, H, D)) / s),
            "hypothesis_mask": bf(_length_weights(B, H))}


def reference(premise_batch, premise_mask, hypothesis_batch, hypothesis_mask):
    p, h = f64(premise_batch), f64(hypothesis_batch)
    d = h.shape[-1]
    sim = (mxq(p, 2, "e4m3") @ mxq(h, 2, "e4m3").transpose(0, 2, 1)) / np.sqrt(float(d))
    kmask = f64(hypothesis_mask)[:, None, :]
    z = sim * kmask
    e = np.exp(z - z.max(-1, keepdims=True))
    attn = e / e.sum(-1, keepdims=True)
    attn = attn * kmask
    attn = attn / (attn.sum(-1, keepdims=True) + 1e-13)
    out = mxq(attn, 2, "e4m3") @ mxq(h, 1, "e4m3")
    return out * f64(premise_mask)[:, :, None]

@@ -1,0 +1,339 @@
+from contextlib import ExitStack
+import math
+
+import concourse.mybir as mybir
+from concourse.masks import make_identity
+
+F32 = mybir.dt.float32
+BF16 = mybir.dt.bfloat16
+U32 = mybir.dt.uint32
+U8 = mybir.dt.uint8
+FP8X4 = mybir.dt.float8_e4m3fn_x4
+ACT = mybir.ActivationFunctionType
+ALU = mybir.AluOpType
+AX = mybir.AxisListType
+
+P = 128
+B = 2
+ROWS = 4096
+H = 512
+D = 512
+TILES_PER_BATCH = ROWS // P
+NT = B * TILES_PER_BATCH
+GROUP = 4
+NG = NT // GROUP
+
+FLOPS = 2 * 2 * B * ROWS * H * D
+
+
+def tile_uniattention_t_kernel(
+    tc, premise_batch, premise_mask, hypothesis_batch, hypothesis_mask, out
+):
+    nc = tc.nc
+    with ExitStack() as ctx:
+        const = ctx.enter_context(tc.tile_pool(name="const", bufs=1))
+        work = ctx.enter_context(tc.tile_pool(name="work", bufs=3))
+        psum = ctx.enter_context(tc.psum_pool(name="psum", bufs=1))
+        ctx.enter_context(tc.manual_schedule())
+
+        hyp_view = hypothesis_batch.rearrange("b (q t) d -> b q (t d)", t=4)
+        prem_view = premise_batch.rearrange("b (p i) d -> b p (i d)", i=TILES_PER_BATCH)
+        out_view = out.rearrange("b (p i) d -> b p (i d)", i=TILES_PER_BATCH)
+
+        hs = []
+        for b in range(B):
+            hs_b = const.tile([P, 4 * D], BF16, name="hs%d" % b)
+            hs.append(hs_b)
+        xs = []
+        for g in range(NG):
+            xs_g = const.tile([P, GROUP * D], BF16, name="xs%d" % g)
+            xs.append(xs_g)
+        kmb = const.tile([P, B, 4], BF16)
+        pmb = const.tile([P, B, TILES_PER_BATCH], BF16)
+
+        def load_x(g):
+            b = g // (NG // B)
+            c = g % (NG // B)
+            nc.sync.dma_start(
+                out=xs[g][:], in_=prem_view[b][:, c * GROUP * D : (c + 1) * GROUP * D]
+            )
+
+        nc.sync.dma_start(out=hs[0][:], in_=hyp_view[0])
+        load_x(0)
+        nc.sync.dma_start(out=kmb[:], in_=hypothesis_mask.rearrange("b (q t) -> q b t", t=4))
+        load_x(1)
+        nc.sync.dma_start(out=hs[1][:], in_=hyp_view[1])
+        nc.sync.dma_start(out=pmb[:], in_=premise_mask.rearrange("b (p i) -> p b i", i=TILES_PER_BATCH))
+        for g in range(2, NG):
+            load_x(g)
+
+        ident_f = const.tile([P, P], F32)
+        make_identity(nc, ident_f[:])
+        ident_b = const.tile([P, P], BF16)
+        make_identity(nc, ident_b[:])
+
+        kmf = const.tile([P, B * 4], F32)
+        kms = const.tile([P, B * 4], F32)
+        kml = const.tile([P, B * 4], F32)
+        lnk = const.tile([P, B * 4], F32)
+        pmf = const.tile([P, NT], F32)
+
+        def hyp_mask_columns():
+            nc.vector.tensor_copy(out=kmf[:], in_=kmb[:].rearrange("q b t -> q (b t)"))
+            nc.vector.tensor_scalar(
+                out=kms[:], in0=kmf[:], scalar1=1.0 / math.sqrt(float(D)), scalar2=None, op0=ALU.mult
+            )
+            nc.vector.tensor_scalar(
+                out=kml[:], in0=kmf[:], scalar1=2.0 ** -60, scalar2=None, op0=ALU.max
+            )
+            nc.scalar.activation(out=lnk[:], in_=kml[:], func=ACT.Ln)
+
+        def premise_mask_columns():
+            nc.vector.tensor_copy(out=pmf[:], in_=pmb[:].rearrange("p b i -> p (b i)"))
+
+        negmax = const.tile([P, NT], F32)
+        rowsum = const.tile([P, NT], F32)
+        rnorm = const.tile([P, NT], F32)
+
+        hq1 = []
+        hc1 = []
+        hq2 = []
+        hc2 = []
+        for b in range(B):
+            q1_b = const.tile([P, H], U32, name="hq1_%d" % b, align_bytes=64)
+            c1_b = const.tile([P, H], U8, name="hc1_%d" % b, align_bytes=64)
+            q2_b = const.tile([P, D], U32, name="hq2_%d" % b, align_bytes=64)
+            c2_b = const.tile([P, D], U8, name="hc2_%d" % b, align_bytes=64)
+            hq1.append(q1_b)
+            hc1.append(c1_b)
+            hq2.append(q2_b)
+            hc2.append(c2_b)
+
+        live = {}
+
+        def t1(key, src, pair):
+            pt = psum.tile([P, 2, 2, P], F32, tag="pt", bufs=1)
+            words = src[:].bitcast(F32)
+            for i in range(2):
+                for u in range(2):
+                    c0 = (2 * pair + i) * 256 + u * P
+                    nc.tensor.transpose(pt[:, i, u, :], words[:, c0 : c0 + P], ident_f[:])
+            live[("pt", key, pair)] = pt
+
+        def x3(key, pair, on_vector):
+            if pair == 0:
+                gx = work.tile([P, GROUP * D], BF16, tag="gx", align_bytes=64)
+                live[("gx", key)] = gx
+            gx = live[("gx", key)]
+            pt = live[("pt", key, pair)]
+            dst = gx[:].bitcast(F32).rearrange("k (i p u) -> k i p u", i=GROUP, u=2)
+            dst = dst[:, 2 * pair : 2 * pair + 2]
+            src = pt[:].rearrange("k i u p -> k i p u")
+            if on_vector:
+                nc.vector.tensor_copy(out=dst, in_=src)
+            else:
+                nc.scalar.copy(out=dst, in_=src)
+
+        def quantise(key, codes, scales):
+            nc.vector.quantize_mx(
+                out=codes[:].bitcast(FP8X4), scales=scales[:], in_=live[("gx", key)][:]
+            )
+
+        def q1(g):
+            xq = work.tile([P, GROUP * P], U32, tag="xq", align_bytes=64)
+            xc = work.tile([P, GROUP * P], U8, tag="xc", align_bytes=64)
+            quantise(("x", g), xq, xc)
+            live[("xq", g)] = (xq, xc)
+
+        def hyp_position_operand(b):
+            g2 = work.tile([P, 4 * D], BF16, tag="gx", align_bytes=64)
+            nc.vector.tensor_copy(
+                out=g2[:].rearrange("q (c i t) -> q c t i", i=4, t=4),
+                in_=hs[b][:].rearrange("q (t c i) -> q c t i", t=4, i=4),
+            )
+            live[("gx", ("h2", b))] = g2
+
+        def m1(k):
+            g = k // 4
+            t = k % 4
+            b = g // (NG // B)
+            xq, xc = live[("xq", g)]
+            st = psum.tile([P, GROUP * P], F32, tag="st", bufs=2)
+            nc.tensor.matmul_mx(
+                out=st[:],
+                lhsT=hq1[b][:, t * P : (t + 1) * P].bitcast(FP8X4),
+                lhsT_scale=hc1[b][:, t * P : (t + 1) * P],
+                rhs=xq[:].bitcast(FP8X4),
+                rhs_scale=xc[:],
+                start=True,
+                stop=True,
+            )
+            live[("st", k)] = st
+
+        def pa(k):
+            g = k // 4
+            t = k % 4
+            b = g // (NG // B)
+            if t == 0:
+                wt = work.tile([P, 4, GROUP * P], F32, tag="wt")
+                live[("wt", g)] = wt
+            wt = live[("wt", g)]
+            col = b * 4 + t
+            nc.scalar.activation(
+                out=wt[:, t, :],
+                in_=live[("st", k)][:],
+                func=ACT.Identity,
+                bias=lnk[:, col : col + 1],
+                scale=kms[:, col : col + 1],
+            )
+
+        def t2(j):
+            g = j // GROUP
+            i = j % GROUP
+            wt = live[("wt", g)]
+            w = psum.tile([P, H], F32, tag="w", bufs=2)
+            for t in range(4):
+                nc.tensor.transpose(
+                    w[:, t * P : (t + 1) * P], wt[:, t, i * P : (i + 1) * P], ident_f[:]
+                )
+            live[("w", j)] = w
+
+        def pb(j):
+            nc.vector.tensor_reduce(
+                out=negmax[:, j : j + 1], in_=live[("w", j)][:], axis=AX.X, op=ALU.max, negate=True
+            )
+
+        def pc(j):
+            a = work.tile([P, H], F32, tag="a")
+            nc.scalar.activation(
+                out=a[:],
+                in_=live[("w", j)][:],
+                func=ACT.Exp,
+                bias=negmax[:, j : j + 1],
+                scale=1.0,
+                accum_out=rowsum[:, j : j + 1],
+            )
+            live[("a", j)] = a
+
+        def v4(j):
+            nc.vector.reciprocal(out=rnorm[:, j : j + 1], in_=rowsum[:, j : j + 1])
+            attn = work.tile([P, H], BF16, tag="attn")
+            nc.vector.tensor_scalar(
+                out=attn[:], in0=live[("a", j)][:], scalar1=rnorm[:, j : j + 1], scalar2=None, op0=ALU.mult
+            )
+            live[("attn", j)] = attn
+
+        def t3(j):
+            attn = live[("attn", j)]
+            at = psum.tile([P, 4, P], BF16, tag="at", bufs=1)
+            for t in range(4):
+                nc.tensor.transpose(at[:, t, :], attn[:, t * P : (t + 1) * P], ident_b[:])
+            live[("at", j)] = at
+
+        def x1(j):
+            ga = work.tile([P, H], BF16, tag="ga", align_bytes=64)
+            nc.vector.tensor_copy(
+                out=ga[:].rearrange("q (p t) -> q p t", t=4),
+                in_=live[("at", j)][:].rearrange("q t p -> q p t"),
+            )
+            live[("ga", j)] = ga
+
+        def q2(j):
+            aq = work.tile([P, P], U32, tag="aq", align_bytes=64)
+            ac = work.tile([P, P], U8, tag="ac", align_bytes=64)
+            nc.vector.quantize_mx(out=aq[:].bitcast(FP8X4), scales=ac[:], in_=live[("ga", j)][:])
+            live[("aq", j)] = (aq, ac)
+
+        def m2(j):
+            b = j // TILES_PER_BATCH
+            aq, ac = live[("aq", j)]
+            o = psum.tile([P, D], F32, tag="o", bufs=2)
+            nc.tensor.matmul_mx(
+                out=o[:],
+                lhsT=aq[:].bitcast(FP8X4),
+                lhsT_scale=ac[:],
+                rhs=hq2[b][:].bitcast(FP8X4),
+                rhs_scale=hc2[b][:],
+                start=True,
+                stop=True,
+            )
+            live[("o", j)] = o
+
+        def x2(j):
+            g = j // GROUP
+            i = j % GROUP
+            if i == 0:
+                osb = work.tile([P, GROUP * D], F32, tag="osb")
+                live[("osb", g)] = osb
+            osb = live[("osb", g)]
+            nc.scalar.activation(
+                out=osb[:, i * D : (i + 1) * D],
+                in_=live[("o", j)][:],
+                func=ACT.Copy,
+                scale=pmf[:, j : j + 1],
+            )
+            if i == GROUP - 1:
+                b = g // (NG // B)
+                c = g % (NG // B)
+                nc.sync.dma_start(
+                    out=out_view[b][:, c * GROUP * D : (c + 1) * GROUP * D], in_=osb[:]
+                )
+
+        t1(("h1", 0), hs[0], 0)
+        x3(("h1", 0), 0, True)
+        t1(("h1", 0), hs[0], 1)
+        x3(("h1", 0), 1, False)
+
+        def ok(j):
+            return 0 <= j < NT
+
+        for n in range(NT + 16):
+            if ok(n - 12):
+                v4(n - 12)
+            if ok(n - 14):
+                q2(n - 14)
+            if n == 0:
+                quantise(("h1", 0), hq1[0], hc1[0])
+            if n >= 4 and n % 4 == 0 and n // 4 - 1 < NG:
+                q1(n // 4 - 1)
+            if n == 3:
+                quantise(("h2", 0), hq2[0], hc2[0])
+            if n == 9:
+                quantise(("h1", 1), hq1[1], hc1[1])
+            if n == 11:
+                quantise(("h2", 1), hq2[1], hc2[1])
+            if ok(n - 10):
+                t2(n - 10)
+            if ok(n - 13):
+                t3(n - 13)
+            m = n - 1
+            if m >= 0 and m % 2 == 0 and m // 2 < NT // 2:
+                x3(("x", m // 4), (m // 2) % 2, (m // 2) % 2 == 1)
+            if n == 6 or n == 8:
+                x3(("h1", 1), (n - 6) // 2, True)
+            if n == 1:
+                hyp_position_operand(0)
+            if n == 2:
+                hyp_mask_columns()
+            if n == 10:
+                hyp_position_operand(1)
+            if n == 12:
+                premise_mask_columns()
+            if n % 2 == 0 and n // 2 < NT // 2:
+                t1(("x", n // 4), xs[n // 4], (n // 2) % 2)
+            if n == 5 or n == 7:
+                t1(("h1", 1), hs[1], (n - 5) // 2)
+            if ok(n - 15):
+                x2(n - 15)
+            if ok(n - 6):
+                pa(n - 6)
+            if ok(n - 10):
+                pb(n - 10)
+            if ok(n - 11):
+                pc(n - 11)
+            if ok(n - 13):
+                x1(n - 13)
+            if ok(n - 14):
+                m2(n - 14)
+            if ok(n - 5):
+                m1(n - 5)

@@ -22,6 +22,7 @@ TILES_PER_BATCH = ROWS // P
 NT = B * TILES_PER_BATCH
 GROUP = 4
 NG = NT // GROUP
+NP = NT // 2
 
 FLOPS = 2 * 2 * B * ROWS * H * D
 
@@ -60,9 +61,9 @@ def tile_uniattention_t_kernel(
 
         nc.sync.dma_start(out=hs[0][:], in_=hyp_view[0])
         load_x(0)
+        nc.sync.dma_start(out=hs[1][:], in_=hyp_view[1])
         nc.sync.dma_start(out=kmb[:], in_=hypothesis_mask.rearrange("b (q t) -> q b t", t=4))
         load_x(1)
-        nc.sync.dma_start(out=hs[1][:], in_=hyp_view[1])
         nc.sync.dma_start(out=pmb[:], in_=premise_mask.rearrange("b (p i) -> p b i", i=TILES_PER_BATCH))
         for g in range(2, NG):
             load_x(g)
@@ -91,10 +92,6 @@ def tile_uniattention_t_kernel(
         def premise_mask_columns():
             nc.vector.tensor_copy(out=pmf[:], in_=pmb[:].rearrange("p b i -> p (b i)"))
 
-        negmax = const.tile([P, NT], F32)
-        rowsum = const.tile([P, NT], F32)
-        rnorm = const.tile([P, NT], F32)
-
         hq1 = []
         hc1 = []
         hq2 = []
@@ -111,8 +108,8 @@ def tile_uniattention_t_kernel(
 
         live = {}
 
-        def t1(key, src, pair):
-            pt = psum.tile([P, 2, 2, P], F32, tag="pt", bufs=1)
+        def t1(key, src, pair, tag):
+            pt = psum.tile([P, 2, 2, P], F32, tag=tag, bufs=(1 if tag == "pt" else 2))
             words = src[:].bitcast(F32)
             for i in range(2):
                 for u in range(2):
@@ -122,7 +119,7 @@ def tile_uniattention_t_kernel(
 
         def x3(key, pair, on_vector):
             if pair == 0:
-                gx = work.tile([P, GROUP * D], BF16, tag="gx", align_bytes=64)
+                gx = work.tile([P, GROUP * D], BF16, tag="gx", bufs=4, align_bytes=64)
                 live[("gx", key)] = gx
             gx = live[("gx", key)]
             pt = live[("pt", key, pair)]
@@ -146,7 +143,7 @@ def tile_uniattention_t_kernel(
             live[("xq", g)] = (xq, xc)
 
         def hyp_position_operand(b):
-            g2 = work.tile([P, 4 * D], BF16, tag="gx", align_bytes=64)
+            g2 = work.tile([P, 4 * D], BF16, tag="gx", bufs=4, align_bytes=64)
             nc.vector.tensor_copy(
                 out=g2[:].rearrange("q (c i t) -> q c t i", i=4, t=4),
                 in_=hs[b][:].rearrange("q (t c i) -> q c t i", t=4, i=4),
@@ -198,60 +195,71 @@ def tile_uniattention_t_kernel(
                 )
             live[("w", j)] = w
 
-        def pb(j):
-            nc.vector.tensor_reduce(
-                out=negmax[:, j : j + 1], in_=live[("w", j)][:], axis=AX.X, op=ALU.max, negate=True
-            )
+        def pb(p):
+            negmax = work.tile([P, 2], F32, tag="negmax", bufs=4)
+            for i in range(2):
+                nc.vector.tensor_reduce(
+                    out=negmax[:, i : i + 1], in_=live[("w", 2 * p + i)][:], axis=AX.X, op=ALU.max, negate=True
+                )
+            live[("negmax", p)] = negmax
 
-        def pc(j):
-            a = work.tile([P, H], F32, tag="a")
-            nc.scalar.activation(
-                out=a[:],
-                in_=live[("w", j)][:],
-                func=ACT.Exp,
-                bias=negmax[:, j : j + 1],
-                scale=1.0,
-                accum_out=rowsum[:, j : j + 1],
-            )
-            live[("a", j)] = a
+        def pc(p):
+            rowsum = work.tile([P, 2], F32, tag="rowsum", bufs=4)
+            negmax = live[("negmax", p)]
+            for i in range(2):
+                a = work.tile([P, H], F32, tag="a", bufs=4)
+                nc.scalar.activation(
+                    out=a[:],
+                    in_=live[("w", 2 * p + i)][:],
+                    func=ACT.Exp,
+                    bias=negmax[:, i : i + 1],
+                    scale=1.0,
+                    accum_out=rowsum[:, i : i + 1],
+                )
+                live[("a", 2 * p + i)] = a
+            live[("rowsum", p)] = rowsum
 
-        def v4(j):
-            nc.vector.reciprocal(out=rnorm[:, j : j + 1], in_=rowsum[:, j : j + 1])
-            attn = work.tile([P, H], BF16, tag="attn")
-            nc.vector.tensor_scalar(
-                out=attn[:], in0=live[("a", j)][:], scalar1=rnorm[:, j : j + 1], scalar2=None, op0=ALU.mult
-            )
-            live[("attn", j)] = attn
+        def v4(p):
+            rnorm = work.tile([P, 2], F32, tag="rnorm", bufs=4)
+            nc.vector.reciprocal(out=rnorm[:], in_=live[("rowsum", p)][:])
+            for i in range(2):
+                attn = work.tile([P, H], BF16, tag="attn", bufs=4)
+                nc.vector.tensor_scalar(
+                    out=attn[:], in0=live[("a", 2 * p + i)][:], scalar1=rnorm[:, i : i + 1], scalar2=None, op0=ALU.mult
+                )
+                live[("attn", 2 * p + i)] = attn
 
-        def t3(j):
-            attn = live[("attn", j)]
-            at = psum.tile([P, 4, P], BF16, tag="at", bufs=1)
-            for t in range(4):
-                nc.tensor.transpose(at[:, t, :], attn[:, t * P : (t + 1) * P], ident_b[:])
-            live[("at", j)] = at
+        def t3(p):
+            at = psum.tile([P, 2, 4, P], BF16, tag="at", bufs=1)
+            for i in range(2):
+                attn = live[("attn", 2 * p + i)]
+                for t in range(4):
+                    nc.tensor.transpose(at[:, i, t, :], attn[:, t * P : (t + 1) * P], ident_b[:])
+            live[("at", p)] = at
 
-        def x1(j):
-            ga = work.tile([P, H], BF16, tag="ga", align_bytes=64)
+        def x1(p):
+            ga = work.tile([P, 2 * H], BF16, tag="ga", align_bytes=64)
             nc.vector.tensor_copy(
-                out=ga[:].rearrange("q (p t) -> q p t", t=4),
-                in_=live[("at", j)][:].rearrange("q t p -> q p t"),
+                out=ga[:].rearrange("q (i p t) -> q i p t", i=2, t=4),
+                in_=live[("at", p)][:].rearrange("q i t p -> q i p t"),
             )
-            live[("ga", j)] = ga
+            live[("ga", p)] = ga
 
-        def q2(j):
-            aq = work.tile([P, P], U32, tag="aq", align_bytes=64)
-            ac = work.tile([P, P], U8, tag="ac", align_bytes=64)
-            nc.vector.quantize_mx(out=aq[:].bitcast(FP8X4), scales=ac[:], in_=live[("ga", j)][:])
-            live[("aq", j)] = (aq, ac)
+        def q2(p):
+            aq = work.tile([P, 2 * P], U32, tag="aq", align_bytes=64)
+            ac = work.tile([P, 2 * P], U8, tag="ac", align_bytes=64)
+            nc.vector.quantize_mx(out=aq[:].bitcast(FP8X4), scales=ac[:], in_=live[("ga", p)][:])
+            live[("aq", p)] = (aq, ac)
 
         def m2(j):
             b = j // TILES_PER_BATCH
-            aq, ac = live[("aq", j)]
+            aq, ac = live[("aq", j // 2)]
+            i = j % 2
             o = psum.tile([P, D], F32, tag="o", bufs=2)
             nc.tensor.matmul_mx(
                 out=o[:],
-                lhsT=aq[:].bitcast(FP8X4),
-                lhsT_scale=ac[:],
+                lhsT=aq[:, i * P : (i + 1) * P].bitcast(FP8X4),
+                lhsT_scale=ac[:, i * P : (i + 1) * P],
                 rhs=hq2[b][:].bitcast(FP8X4),
                 rhs_scale=hc2[b][:],
                 start=True,
@@ -279,61 +287,61 @@ def tile_uniattention_t_kernel(
                     out=out_view[b][:, c * GROUP * D : (c + 1) * GROUP * D], in_=osb[:]
                 )
 
-        t1(("h1", 0), hs[0], 0)
+        t1(("h1", 0), hs[0], 0, "o")
+        t1(("h1", 0), hs[0], 1, "o")
         x3(("h1", 0), 0, True)
-        t1(("h1", 0), hs[0], 1)
         x3(("h1", 0), 1, False)
+        quantise(("h1", 0), hq1[0], hc1[0])
 
-        def ok(j):
-            return 0 <= j < NT
+        def ok(p):
+            return 0 <= p < NP
 
-        for n in range(NT + 16):
-            if ok(n - 12):
-                v4(n - 12)
-            if ok(n - 14):
-                q2(n - 14)
-            if n == 0:
-                quantise(("h1", 0), hq1[0], hc1[0])
-            if n >= 4 and n % 4 == 0 and n // 4 - 1 < NG:
-                q1(n // 4 - 1)
-            if n == 3:
-                quantise(("h2", 0), hq2[0], hc2[0])
-            if n == 9:
-                quantise(("h1", 1), hq1[1], hc1[1])
-            if n == 11:
-                quantise(("h2", 1), hq2[1], hc2[1])
-            if ok(n - 10):
-                t2(n - 10)
-            if ok(n - 13):
-                t3(n - 13)
-            m = n - 1
-            if m >= 0 and m % 2 == 0 and m // 2 < NT // 2:
-                x3(("x", m // 4), (m // 2) % 2, (m // 2) % 2 == 1)
-            if n == 6 or n == 8:
-                x3(("h1", 1), (n - 6) // 2, True)
-            if n == 1:
+        for r in range(NP + 9):
+            if ok(r - 6):
+                pc(r - 6)
+            if ok(r - 7):
+                x1(r - 7)
+            if ok(r - 5):
+                t2(2 * (r - 5))
+                t2(2 * (r - 5) + 1)
+            if ok(r - 6):
+                v4(r - 6)
+                t3(r - 6)
+            if ok(r - 8):
+                x2(2 * (r - 8))
+                x2(2 * (r - 8) + 1)
+            if ok(r - 1):
+                x3(("x", (r - 1) // 2), (r - 1) % 2, (r - 1) % 2 == 1)
+            if r == 2 or r == 3:
+                t1(("h1", 1), hs[1], r - 2, "o")
+                x3(("h1", 1), r - 2, False)
+            if r == 0:
                 hyp_position_operand(0)
-            if n == 2:
+            if r == 2:
                 hyp_mask_columns()
-            if n == 10:
                 hyp_position_operand(1)
-            if n == 12:
+            if r == 6:
                 premise_mask_columns()
-            if n % 2 == 0 and n // 2 < NT // 2:
-                t1(("x", n // 4), xs[n // 4], (n // 2) % 2)
-            if n == 5 or n == 7:
-                t1(("h1", 1), hs[1], (n - 5) // 2)
-            if ok(n - 15):
-                x2(n - 15)
-            if ok(n - 6):
-                pa(n - 6)
-            if ok(n - 10):
-                pb(n - 10)
-            if ok(n - 11):
-                pc(n - 11)
-            if ok(n - 13):
-                x1(n - 13)
-            if ok(n - 14):
-                m2(n - 14)
-            if ok(n - 5):
-                m1(n - 5)
+            if ok(r):
+                t1(("x", r // 2), xs[r // 2], r % 2, "pt")
+            if ok(r - 7):
+                q2(r - 7)
+            if r >= 3 and r % 2 == 1 and (r - 3) // 2 < NG:
+                q1((r - 3) // 2)
+            if r == 2:
+                quantise(("h2", 0), hq2[0], hc2[0])
+            if r == 4:
+                quantise(("h2", 1), hq2[1], hc2[1])
+            if r == 5:
+                quantise(("h1", 1), hq1[1], hc1[1])
+            if ok(r - 7):
+                m2(2 * (r - 7))
+                m2(2 * (r - 7) + 1)
+            if ok(r - 3):
+                m1(2 * (r - 3))
+                m1(2 * (r - 3) + 1)
+            if ok(r - 5):
+                pb(r - 5)
+            if ok(r - 3):
+                pa(2 * (r - 3))
+                pa(2 * (r - 3) + 1)

@@ -119,7 +119,9 @@ def tile_uniattention_t_kernel(
 
         def x3(key, pair, on_vector):
             if pair == 0:
-                gx = work.tile([P, GROUP * D], BF16, tag="gx", bufs=4, align_bytes=64)
+                gx = work.tile(
+                    [P, GROUP * D], BF16, tag=("gx" if key[0] == "x" else "gh"), bufs=4, align_bytes=64
+                )
                 live[("gx", key)] = gx
             gx = live[("gx", key)]
             pt = live[("pt", key, pair)]
@@ -143,7 +145,7 @@ def tile_uniattention_t_kernel(
             live[("xq", g)] = (xq, xc)
 
         def hyp_position_operand(b):
-            g2 = work.tile([P, 4 * D], BF16, tag="gx", bufs=4, align_bytes=64)
+            g2 = work.tile([P, 4 * D], BF16, tag="gh", bufs=4, align_bytes=64)
             nc.vector.tensor_copy(
                 out=g2[:].rearrange("q (c i t) -> q c t i", i=4, t=4),
                 in_=hs[b][:].rearrange("q (t c i) -> q c t i", t=4, i=4),
@@ -167,7 +169,7 @@ def tile_uniattention_t_kernel(
             )
             live[("st", k)] = st
 
-        def pa(k):
+        def pa(k, on_vector):
             g = k // 4
             t = k % 4
             b = g // (NG // B)
@@ -176,13 +178,23 @@ def tile_uniattention_t_kernel(
                 live[("wt", g)] = wt
             wt = live[("wt", g)]
             col = b * 4 + t
-            nc.scalar.activation(
-                out=wt[:, t, :],
-                in_=live[("st", k)][:],
-                func=ACT.Identity,
-                bias=lnk[:, col : col + 1],
-                scale=kms[:, col : col + 1],
-            )
+            if on_vector:
+                nc.vector.tensor_scalar(
+                    out=wt[:, t, :],
+                    in0=live[("st", k)][:],
+                    scalar1=kms[:, col : col + 1],
+                    scalar2=lnk[:, col : col + 1],
+                    op0=ALU.mult,
+                    op1=ALU.add,
+                )
+            else:
+                nc.scalar.activation(
+                    out=wt[:, t, :],
+                    in_=live[("st", k)][:],
+                    func=ACT.Identity,
+                    bias=lnk[:, col : col + 1],
+                    scale=kms[:, col : col + 1],
+                )
 
         def t2(j):
             g = j // GROUP
@@ -195,37 +207,45 @@ def tile_uniattention_t_kernel(
                 )
             live[("w", j)] = w
 
-        def pb(p):
-            negmax = work.tile([P, 2], F32, tag="negmax", bufs=4)
-            for i in range(2):
-                nc.vector.tensor_reduce(
-                    out=negmax[:, i : i + 1], in_=live[("w", 2 * p + i)][:], axis=AX.X, op=ALU.max, negate=True
-                )
-            live[("negmax", p)] = negmax
+        def pb(j):
+            p = j // 2
+            i = j % 2
+            if i == 0:
+                negmax = work.tile([P, 2], F32, tag="negmax", bufs=4)
+                live[("negmax", p)] = negmax
+            nc.vector.tensor_reduce(
+                out=live[("negmax", p)][:, i : i + 1], in_=live[("w", j)][:], axis=AX.X, op=ALU.max, negate=True
+            )
 
-        def pc(p):
-            rowsum = work.tile([P, 2], F32, tag="rowsum", bufs=4)
-            negmax = live[("negmax", p)]
-            for i in range(2):
-                a = work.tile([P, H], F32, tag="a", bufs=4)
-                nc.scalar.activation(
-                    out=a[:],
-                    in_=live[("w", 2 * p + i)][:],
-                    func=ACT.Exp,
-                    bias=negmax[:, i : i + 1],
-                    scale=1.0,
-                    accum_out=rowsum[:, i : i + 1],
-                )
-                live[("a", 2 * p + i)] = a
-            live[("rowsum", p)] = rowsum
+        def pc(j):
+            p = j // 2
+            i = j % 2
+            if i == 0:
+                rowsum = work.tile([P, 2], F32, tag="rowsum", bufs=4)
+                live[("rowsum", p)] = rowsum
+            a = work.tile([P, H], F32, tag="a", bufs=4)
+            nc.scalar.activation(
+                out=a[:],
+                in_=live[("w", j)][:],
+                func=ACT.Exp,
+                bias=live[("negmax", p)][:, i : i + 1],
+                scale=1.0,
+                accum_out=live[("rowsum", p)][:, i : i + 1],
+            )
+            live[("a", j)] = a
 
         def v4(p):
             rnorm = work.tile([P, 2], F32, tag="rnorm", bufs=4)
             nc.vector.reciprocal(out=rnorm[:], in_=live[("rowsum", p)][:])
             for i in range(2):
                 attn = work.tile([P, H], BF16, tag="attn", bufs=4)
-                nc.vector.tensor_scalar(
-                    out=attn[:], in0=live[("a", 2 * p + i)][:], scalar1=rnorm[:, i : i + 1], scalar2=None, op0=ALU.mult
+                nc.gpsimd.tensor_scalar(
+                    out=attn[:],
+                    in0=live[("a", 2 * p + i)][:],
+                    scalar1=rnorm[:, i : i + 1],
+                    scalar2=0.0,
+                    op0=ALU.mult,
+                    op1=ALU.add,
                 )
                 live[("attn", 2 * p + i)] = attn
 
@@ -267,25 +287,36 @@ def tile_uniattention_t_kernel(
             )
             live[("o", j)] = o
 
-        def x2(j):
-            g = j // GROUP
-            i = j % GROUP
+        def x2(j, on_vector):
+            p = j // 2
+            i = j % 2
             if i == 0:
-                osb = work.tile([P, GROUP * D], F32, tag="osb")
-                live[("osb", g)] = osb
-            osb = live[("osb", g)]
-            nc.scalar.activation(
-                out=osb[:, i * D : (i + 1) * D],
-                in_=live[("o", j)][:],
-                func=ACT.Copy,
-                scale=pmf[:, j : j + 1],
-            )
-            if i == GROUP - 1:
-                b = g // (NG // B)
-                c = g % (NG // B)
-                nc.sync.dma_start(
-                    out=out_view[b][:, c * GROUP * D : (c + 1) * GROUP * D], in_=osb[:]
+                osb = work.tile([P, 2 * D], F32, tag="osb", bufs=4)
+                live[("osb", p)] = osb
+            osb = live[("osb", p)]
+            if on_vector:
+                nc.vector.tensor_scalar(
+                    out=osb[:, i * D : (i + 1) * D],
+                    in0=live[("o", j)][:],
+                    scalar1=pmf[:, j : j + 1],
+                    scalar2=None,
+                    op0=ALU.mult,
                 )
+            else:
+                nc.scalar.activation(
+                    out=osb[:, i * D : (i + 1) * D],
+                    in_=live[("o", j)][:],
+                    func=ACT.Copy,
+                    scale=pmf[:, j : j + 1],
+                )
+            b = j // TILES_PER_BATCH
+            c = j % TILES_PER_BATCH
+            if p == NP - 1:
+                nc.sync.dma_start(
+                    out=out_view[b][:, c * D : (c + 1) * D], in_=osb[:, i * D : (i + 1) * D]
+                )
+            elif i == 1:
+                nc.sync.dma_start(out=out_view[b][:, (c - 1) * D : (c + 1) * D], in_=osb[:])
 
         t1(("h1", 0), hs[0], 0, "o")
         t1(("h1", 0), hs[0], 1, "o")
@@ -296,25 +327,65 @@ def tile_uniattention_t_kernel(
         def ok(p):
             return 0 <= p < NP
 
-        for r in range(NP + 9):
-            if ok(r - 6):
-                pc(r - 6)
-            if ok(r - 7):
-                x1(r - 7)
-            if ok(r - 5):
-                t2(2 * (r - 5))
-                t2(2 * (r - 5) + 1)
-            if ok(r - 6):
-                v4(r - 6)
-                t3(r - 6)
-            if ok(r - 8):
-                x2(2 * (r - 8))
-                x2(2 * (r - 8) + 1)
-            if ok(r - 1):
-                x3(("x", (r - 1) // 2), (r - 1) % 2, (r - 1) % 2 == 1)
+        def pa_on_vector(k):
+            return k % 8 == 5
+
+        def x2_on_vector(j):
+            return j == NT - 1
+
+        def x3_on_vector(p):
+            return p >= 3
+
+        for r in range(NP + 12):
+            if ok(r - 1) and not x3_on_vector(r - 1):
+                x3(("x", (r - 1) // 2), (r - 1) % 2, False)
+            for i in range(2):
+                if ok(r - 7):
+                    pc(2 * (r - 7) + i)
+                if ok(r - 11) and not x2_on_vector(2 * (r - 11) + i):
+                    x2(2 * (r - 11) + i, False)
+                if ok(r - 4) and not pa_on_vector(2 * (r - 4) + i):
+                    pa(2 * (r - 4) + i, False)
+            if ok(r - 4) and pa_on_vector(2 * (r - 4) + 1):
+                pa(2 * (r - 4) + 1, True)
+            if ok(r - 1) and x3_on_vector(r - 1):
+                x3(("x", (r - 1) // 2), (r - 1) % 2, True)
             if r == 2 or r == 3:
                 t1(("h1", 1), hs[1], r - 2, "o")
+            if ok(r - 6):
+                t2(2 * (r - 6))
+            if ok(r - 9):
+                t3(r - 9)
+            if ok(r - 10):
+                m2(2 * (r - 10))
+            if ok(r - 6):
+                t2(2 * (r - 6) + 1)
+            if ok(r - 3):
+                m1(2 * (r - 3))
+            if ok(r - 10):
+                m2(2 * (r - 10) + 1)
+            if ok(r - 3):
+                m1(2 * (r - 3) + 1)
+            if ok(r):
+                t1(("x", r // 2), xs[r // 2], r % 2, "pt")
+            if r == 2 or r == 3:
                 x3(("h1", 1), r - 2, False)
+            if ok(r - 6):
+                pb(2 * (r - 6))
+            if ok(r - 9):
+                x1(r - 9)
+            if ok(r - 6):
+                pb(2 * (r - 6) + 1)
+            if r >= 2 and r % 2 == 0 and (r - 2) // 2 < NG:
+                q1((r - 2) // 2)
+            if r == 2:
+                quantise(("h2", 0), hq2[0], hc2[0])
+            if r == 4:
+                quantise(("h2", 1), hq2[1], hc2[1])
+            if r == 5:
+                quantise(("h1", 1), hq1[1], hc1[1])
+            if ok(r - 11) and x2_on_vector(2 * (r - 11) + 1):
+                x2(2 * (r - 11) + 1, True)
             if r == 0:
                 hyp_position_operand(0)
             if r == 2:
@@ -322,26 +393,7 @@ def tile_uniattention_t_kernel(
                 hyp_position_operand(1)
             if r == 6:
                 premise_mask_columns()
-            if ok(r):
-                t1(("x", r // 2), xs[r // 2], r % 2, "pt")
+            if ok(r - 9):
+                q2(r - 9)
             if ok(r - 7):
-                q2(r - 7)
-            if r >= 3 and r % 2 == 1 and (r - 3) // 2 < NG:
-                q1((r - 3) // 2)
-            if r == 2:
-                quantise(("h2", 0), hq2[0], hc2[0])
-            if r == 4:
-                quantise(("h2", 1), hq2[1], hc2[1])
-            if r == 5:
-                quantise(("h1", 1), hq1[1], hc1[1])
-            if ok(r - 7):
-                m2(2 * (r - 7))
-                m2(2 * (r - 7) + 1)
-            if ok(r - 3):
-                m1(2 * (r - 3))
-                m1(2 * (r - 3) + 1)
-            if ok(r - 5):
-                pb(r - 5)
-            if ok(r - 3):
-                pa(2 * (r - 3))
-                pa(2 * (r - 3) + 1)
+                v4(r - 7)

@@ -173,10 +173,10 @@ def tile_uniattention_t_kernel(
             g = k // 4
             t = k % 4
             b = g // (NG // B)
-            if t == 0:
+            wt = live.get(("wt", g))
+            if wt is None:
                 wt = work.tile([P, 4, GROUP * P], F32, tag="wt")
                 live[("wt", g)] = wt
-            wt = live[("wt", g)]
             col = b * 4 + t
             if on_vector:
                 nc.vector.tensor_scalar(
@@ -328,7 +328,9 @@ def tile_uniattention_t_kernel(
             return 0 <= p < NP
 
         def pa_on_vector(k):
-            return k % 8 == 5
+            if k >= 56:
+                return k % 3 == 0
+            return k % 6 == 0
 
         def x2_on_vector(j):
             return j == NT - 1
@@ -339,35 +341,53 @@ def tile_uniattention_t_kernel(
         for r in range(NP + 12):
             if ok(r - 1) and not x3_on_vector(r - 1):
                 x3(("x", (r - 1) // 2), (r - 1) % 2, False)
+            if ok(r - 7):
+                pc(2 * (r - 7))
+            if ok(r - 11):
+                x2(2 * (r - 11), False)
+            if ok(r - 4) and not pa_on_vector(2 * (r - 4)):
+                pa(2 * (r - 4), False)
+            if ok(r - 7):
+                pc(2 * (r - 7) + 1)
+            if ok(r - 4) and not pa_on_vector(2 * (r - 4) + 1):
+                pa(2 * (r - 4) + 1, False)
+            if ok(r - 11) and not x2_on_vector(2 * (r - 11) + 1):
+                x2(2 * (r - 11) + 1, False)
+            if r == 2:
+                quantise(("h2", 0), hq2[0], hc2[0])
+            if r == 4:
+                quantise(("h2", 1), hq2[1], hc2[1])
+            if r == 5:
+                quantise(("h1", 1), hq1[1], hc1[1])
+            if r == 0:
+                hyp_position_operand(0)
+            if r == 2:
+                hyp_mask_columns()
+                hyp_position_operand(1)
+            if r == 6:
+                premise_mask_columns()
             for i in range(2):
-                if ok(r - 7):
-                    pc(2 * (r - 7) + i)
-                if ok(r - 11) and not x2_on_vector(2 * (r - 11) + i):
-                    x2(2 * (r - 11) + i, False)
-                if ok(r - 4) and not pa_on_vector(2 * (r - 4) + i):
-                    pa(2 * (r - 4) + i, False)
-            if ok(r - 4) and pa_on_vector(2 * (r - 4) + 1):
-                pa(2 * (r - 4) + 1, True)
+                if ok(r - 4) and pa_on_vector(2 * (r - 4) + i):
+                    pa(2 * (r - 4) + i, True)
             if ok(r - 1) and x3_on_vector(r - 1):
                 x3(("x", (r - 1) // 2), (r - 1) % 2, True)
-            if r == 2 or r == 3:
-                t1(("h1", 1), hs[1], r - 2, "o")
             if ok(r - 6):
                 t2(2 * (r - 6))
             if ok(r - 9):
                 t3(r - 9)
             if ok(r - 10):
                 m2(2 * (r - 10))
+            if r == 2 or r == 3:
+                t1(("h1", 1), hs[1], r - 2, "o")
             if ok(r - 6):
                 t2(2 * (r - 6) + 1)
             if ok(r - 3):
                 m1(2 * (r - 3))
-            if ok(r - 10):
-                m2(2 * (r - 10) + 1)
-            if ok(r - 3):
                 m1(2 * (r - 3) + 1)
             if ok(r):
                 t1(("x", r // 2), xs[r // 2], r % 2, "pt")
+            if ok(r - 10):
+                m2(2 * (r - 10) + 1)
             if r == 2 or r == 3:
                 x3(("h1", 1), r - 2, False)
             if ok(r - 6):
@@ -376,24 +396,11 @@ def tile_uniattention_t_kernel(
                 x1(r - 9)
             if ok(r - 6):
                 pb(2 * (r - 6) + 1)
-            if r >= 2 and r % 2 == 0 and (r - 2) // 2 < NG:
-                q1((r - 2) // 2)
-            if r == 2:
-                quantise(("h2", 0), hq2[0], hc2[0])
-            if r == 4:
-                quantise(("h2", 1), hq2[1], hc2[1])
-            if r == 5:
-                quantise(("h1", 1), hq1[1], hc1[1])
-            if ok(r - 11) and x2_on_vector(2 * (r - 11) + 1):
-                x2(2 * (r - 11) + 1, True)
-            if r == 0:
-                hyp_position_operand(0)
-            if r == 2:
-                hyp_mask_columns()
-                hyp_position_operand(1)
-            if r == 6:
-                premise_mask_columns()
             if ok(r - 9):
                 q2(r - 9)
+            if ok(r - 11) and x2_on_vector(2 * (r - 11) + 1):
+                x2(2 * (r - 11) + 1, True)
+            if r >= 2 and r % 2 == 0 and (r - 2) // 2 < NG:
+                q1((r - 2) // 2)
             if ok(r - 7):
                 v4(r - 7)

@@ -173,10 +173,10 @@ def tile_uniattention_t_kernel(
             g = k // 4
             t = k % 4
             b = g // (NG // B)
-            wt = live.get(("wt", g))
-            if wt is None:
+            if t == 0:
                 wt = work.tile([P, 4, GROUP * P], F32, tag="wt")
                 live[("wt", g)] = wt
+            wt = live[("wt", g)]
             col = b * 4 + t
             if on_vector:
                 nc.vector.tensor_scalar(
@@ -328,9 +328,7 @@ def tile_uniattention_t_kernel(
             return 0 <= p < NP
 
         def pa_on_vector(k):
-            if k >= 56:
-                return k % 3 == 0
-            return k % 6 == 0
+            return False
 
         def x2_on_vector(j):
             return j == NT - 1
@@ -341,53 +339,35 @@ def tile_uniattention_t_kernel(
         for r in range(NP + 12):
             if ok(r - 1) and not x3_on_vector(r - 1):
                 x3(("x", (r - 1) // 2), (r - 1) % 2, False)
-            if ok(r - 7):
-                pc(2 * (r - 7))
-            if ok(r - 11):
-                x2(2 * (r - 11), False)
-            if ok(r - 4) and not pa_on_vector(2 * (r - 4)):
-                pa(2 * (r - 4), False)
-            if ok(r - 7):
-                pc(2 * (r - 7) + 1)
-            if ok(r - 4) and not pa_on_vector(2 * (r - 4) + 1):
-                pa(2 * (r - 4) + 1, False)
-            if ok(r - 11) and not x2_on_vector(2 * (r - 11) + 1):
-                x2(2 * (r - 11) + 1, False)
-            if r == 2:
-                quantise(("h2", 0), hq2[0], hc2[0])
-            if r == 4:
-                quantise(("h2", 1), hq2[1], hc2[1])
-            if r == 5:
-                quantise(("h1", 1), hq1[1], hc1[1])
-            if r == 0:
-                hyp_position_operand(0)
-            if r == 2:
-                hyp_mask_columns()
-                hyp_position_operand(1)
-            if r == 6:
-                premise_mask_columns()
             for i in range(2):
-                if ok(r - 4) and pa_on_vector(2 * (r - 4) + i):
-                    pa(2 * (r - 4) + i, True)
+                if ok(r - 7):
+                    pc(2 * (r - 7) + i)
+                if ok(r - 11) and not x2_on_vector(2 * (r - 11) + i):
+                    x2(2 * (r - 11) + i, False)
+                if ok(r - 4) and not pa_on_vector(2 * (r - 4) + i):
+                    pa(2 * (r - 4) + i, False)
+            if ok(r - 4) and pa_on_vector(2 * (r - 4) + 1):
+                pa(2 * (r - 4) + 1, True)
             if ok(r - 1) and x3_on_vector(r - 1):
                 x3(("x", (r - 1) // 2), (r - 1) % 2, True)
+            if r == 2 or r == 3:
+                t1(("h1", 1), hs[1], r - 2, "o")
             if ok(r - 6):
                 t2(2 * (r - 6))
             if ok(r - 9):
                 t3(r - 9)
             if ok(r - 10):
                 m2(2 * (r - 10))
-            if r == 2 or r == 3:
-                t1(("h1", 1), hs[1], r - 2, "o")
             if ok(r - 6):
                 t2(2 * (r - 6) + 1)
             if ok(r - 3):
                 m1(2 * (r - 3))
+            if ok(r - 10):
+                m2(2 * (r - 10) + 1)
+            if ok(r - 3):
                 m1(2 * (r - 3) + 1)
             if ok(r):
                 t1(("x", r // 2), xs[r // 2], r % 2, "pt")
-            if ok(r - 10):
-                m2(2 * (r - 10) + 1)
             if r == 2 or r == 3:
                 x3(("h1", 1), r - 2, False)
             if ok(r - 6):
@@ -396,11 +376,24 @@ def tile_uniattention_t_kernel(
                 x1(r - 9)
             if ok(r - 6):
                 pb(2 * (r - 6) + 1)
-            if ok(r - 9):
-                q2(r - 9)
-            if ok(r - 11) and x2_on_vector(2 * (r - 11) + 1):
-                x2(2 * (r - 11) + 1, True)
             if r >= 2 and r % 2 == 0 and (r - 2) // 2 < NG:
                 q1((r - 2) // 2)
+            if r == 2:
+                quantise(("h2", 0), hq2[0], hc2[0])
+            if r == 4:
+                quantise(("h2", 1), hq2[1], hc2[1])
+            if r == 5:
+                quantise(("h1", 1), hq1[1], hc1[1])
+            if ok(r - 11) and x2_on_vector(2 * (r - 11) + 1):
+                x2(2 * (r - 11) + 1, True)
+            if r == 0:
+                hyp_position_operand(0)
+            if r == 2:
+                hyp_mask_columns()
+                hyp_position_operand(1)
+            if r == 6:
+                premise_mask_columns()
+            if ok(r - 9):
+                q2(r - 9)
             if ok(r - 7):
                 v4(r - 7)

@@ -35,7 +35,6 @@ def tile_uniattention_t_kernel(
         const = ctx.enter_context(tc.tile_pool(name="const", bufs=1))
         work = ctx.enter_context(tc.tile_pool(name="work", bufs=3))
         psum = ctx.enter_context(tc.psum_pool(name="psum", bufs=1))
-        ctx.enter_context(tc.manual_schedule())
 
         hyp_view = hypothesis_batch.rearrange("b (q t) d -> b q (t d)", t=4)
         prem_view = premise_batch.rearrange("b (p i) d -> b p (i d)", i=TILES_PER_BATCH)
@@ -328,7 +327,7 @@ def tile_uniattention_t_kernel(
             return 0 <= p < NP
 
         def pa_on_vector(k):
-            return False
+            return k % 8 == 5
 
         def x2_on_vector(j):
             return j == NT - 1

from contextlib import ExitStack
import math

import concourse.mybir as mybir
from concourse.masks import make_identity

F32 = mybir.dt.float32
BF16 = mybir.dt.bfloat16
U32 = mybir.dt.uint32
U8 = mybir.dt.uint8
FP8X4 = mybir.dt.float8_e4m3fn_x4
ACT = mybir.ActivationFunctionType
ALU = mybir.AluOpType
AX = mybir.AxisListType

P = 128
B = 2
ROWS = 4096
H = 512
D = 512
TILES_PER_BATCH = ROWS // P
NT = B * TILES_PER_BATCH
GROUP = 4
NG = NT // GROUP
NP = NT // 2

FLOPS = 2 * 2 * B * ROWS * H * D


def tile_uniattention_t_kernel(
    tc, premise_batch, premise_mask, hypothesis_batch, hypothesis_mask, out
):
    nc = tc.nc
    with ExitStack() as ctx:
        const = ctx.enter_context(tc.tile_pool(name="const", bufs=1))
        work = ctx.enter_context(tc.tile_pool(name="work", bufs=3))
        psum = ctx.enter_context(tc.psum_pool(name="psum", bufs=1))

        hyp_view = hypothesis_batch.rearrange("b (q t) d -> b q (t d)", t=4)
        prem_view = premise_batch.rearrange("b (p i) d -> b p (i d)", i=TILES_PER_BATCH)
        out_view = out.rearrange("b (p i) d -> b p (i d)", i=TILES_PER_BATCH)

        hs = []
        for b in range(B):
            hs_b = const.tile([P, 4 * D], BF16, name="hs%d" % b)
            hs.append(hs_b)
        xs = []
        for g in range(NG):
            xs_g = const.tile([P, GROUP * D], BF16, name="xs%d" % g)
            xs.append(xs_g)
        kmb = const.tile([P, B, 4], BF16)
        pmb = const.tile([P, B, TILES_PER_BATCH], BF16)

        def load_x(g):
            b = g // (NG // B)
            c = g % (NG // B)
            nc.sync.dma_start(
                out=xs[g][:], in_=prem_view[b][:, c * GROUP * D : (c + 1) * GROUP * D]
            )

        nc.sync.dma_start(out=hs[0][:], in_=hyp_view[0])
        load_x(0)
        nc.sync.dma_start(out=hs[1][:], in_=hyp_view[1])
        nc.sync.dma_start(out=kmb[:], in_=hypothesis_mask.rearrange("b (q t) -> q b t", t=4))
        load_x(1)
        nc.sync.dma_start(out=pmb[:], in_=premise_mask.rearrange("b (p i) -> p b i", i=TILES_PER_BATCH))
        for g in range(2, NG):
            load_x(g)

        ident_f = const.tile([P, P], F32)
        make_identity(nc, ident_f[:])
        ident_b = const.tile([P, P], BF16)
        make_identity(nc, ident_b[:])

        kmf = const.tile([P, B * 4], F32)
        kms = const.tile([P, B * 4], F32)
        kml = const.tile([P, B * 4], F32)
        lnk = const.tile([P, B * 4], F32)
        pmf = const.tile([P, NT], F32)

        def hyp_mask_columns():
            nc.vector.tensor_copy(out=kmf[:], in_=kmb[:].rearrange("q b t -> q (b t)"))
            nc.vector.tensor_scalar(
                out=kms[:], in0=kmf[:], scalar1=1.0 / math.sqrt(float(D)), scalar2=None, op0=ALU.mult
            )
            nc.vector.tensor_scalar(
                out=kml[:], in0=kmf[:], scalar1=2.0 ** -60, scalar2=None, op0=ALU.max
            )
            nc.scalar.activation(out=lnk[:], in_=kml[:], func=ACT.Ln)

        def premise_mask_columns():
            nc.vector.tensor_copy(out=pmf[:], in_=pmb[:].rearrange("p b i -> p (b i)"))

        hq1 = []
        hc1 = []
        hq2 = []
        hc2 = []
        for b in range(B):
            q1_b = const.tile([P, H], U32, name="hq1_%d" % b, align_bytes=64)
            c1_b = const.tile([P, H], U8, name="hc1_%d" % b, align_bytes=64)
            q2_b = const.tile([P, D], U32, name="hq2_%d" % b, align_bytes=64)
            c2_b = const.tile([P, D], U8, name="hc2_%d" % b, align_bytes=64)
            hq1.append(q1_b)
            hc1.append(c1_b)
            hq2.append(q2_b)
            hc2.append(c2_b)

        live = {}

        def t1(key, src, pair, tag):
            pt = psum.tile([P, 2, 2, P], F32, tag=tag, bufs=(1 if tag == "pt" else 2))
            words = src[:].bitcast(F32)
            for i in range(2):
                for u in range(2):
                    c0 = (2 * pair + i) * 256 + u * P
                    nc.tensor.transpose(pt[:, i, u, :], words[:, c0 : c0 + P], ident_f[:])
            live[("pt", key, pair)] = pt

        def x3(key, pair, on_vector):
            if pair == 0:
                gx = work.tile(
                    [P, GROUP * D], BF16, tag=("gx" if key[0] == "x" else "gh"), bufs=4, align_bytes=64
                )
                live[("gx", key)] = gx
            gx = live[("gx", key)]
            pt = live[("pt", key, pair)]
            dst = gx[:].bitcast(F32).rearrange("k (i p u) -> k i p u", i=GROUP, u=2)
            dst = dst[:, 2 * pair : 2 * pair + 2]
            src = pt[:].rearrange("k i u p -> k i p u")
            if on_vector:
                nc.vector.tensor_copy(out=dst, in_=src)
            else:
                nc.scalar.copy(out=dst, in_=src)

        def quantise(key, codes, scales):
            nc.vector.quantize_mx(
                out=codes[:].bitcast(FP8X4), scales=scales[:], in_=live[("gx", key)][:]
            )

        def q1(g):
            xq = work.tile([P, GROUP * P], U32, tag="xq", align_bytes=64)
            xc = work.tile([P, GROUP * P], U8, tag="xc", align_bytes=64)
            quantise(("x", g), xq, xc)
            live[("xq", g)] = (xq, xc)

        def hyp_position_operand(b):
            g2 = work.tile([P, 4 * D], BF16, tag="gh", bufs=4, align_bytes=64)
            nc.vector.tensor_copy(
                out=g2[:].rearrange("q (c i t) -> q c t i", i=4, t=4),
                in_=hs[b][:].rearrange("q (t c i) -> q c t i", t=4, i=4),
            )
            live[("gx", ("h2", b))] = g2

        def m1(k):
            g = k // 4
            t = k % 4
            b = g // (NG // B)
            xq, xc = live[("xq", g)]
            st = psum.tile([P, GROUP * P], F32, tag="st", bufs=2)
            nc.tensor.matmul_mx(
                out=st[:],
                lhsT=hq1[b][:, t * P : (t + 1) * P].bitcast(FP8X4),
                lhsT_scale=hc1[b][:, t * P : (t + 1) * P],
                rhs=xq[:].bitcast(FP8X4),
                rhs_scale=xc[:],
                start=True,
                stop=True,
            )
            live[("st", k)] = st

        def pa(k, on_vector):
            g = k // 4
            t = k % 4
            b = g // (NG // B)
            if t == 0:
                wt = work.tile([P, 4, GROUP * P], F32, tag="wt")
                live[("wt", g)] = wt
            wt = live[("wt", g)]
            col = b * 4 + t
            if on_vector:
                nc.vector.tensor_scalar(
                    out=wt[:, t, :],
                    in0=live[("st", k)][:],
                    scalar1=kms[:, col : col + 1],
                    scalar2=lnk[:, col : col + 1],
                    op0=ALU.mult,
                    op1=ALU.add,
                )
            else:
                nc.scalar.activation(
                    out=wt[:, t, :],
                    in_=live[("st", k)][:],
                    func=ACT.Identity,
                    bias=lnk[:, col : col + 1],
                    scale=kms[:, col : col + 1],
                )

        def t2(j):
            g = j // GROUP
            i = j % GROUP
            wt = live[("wt", g)]
            w = psum.tile([P, H], F32, tag="w", bufs=2)
            for t in range(4):
                nc.tensor.transpose(
                    w[:, t * P : (t + 1) * P], wt[:, t, i * P : (i + 1) * P], ident_f[:]
                )
            live[("w", j)] = w

        def pb(j):
            p = j // 2
            i = j % 2
            if i == 0:
                negmax = work.tile([P, 2], F32, tag="negmax", bufs=4)
                live[("negmax", p)] = negmax
            nc.vector.tensor_reduce(
                out=live[("negmax", p)][:, i : i + 1], in_=live[("w", j)][:], axis=AX.X, op=ALU.max, negate=True
            )

        def pc(j):
            p = j // 2
            i = j % 2
            if i == 0:
                rowsum = work.tile([P, 2], F32, tag="rowsum", bufs=4)
                live[("rowsum", p)] = rowsum
            a = work.tile([P, H], F32, tag="a", bufs=4)
            nc.scalar.activation(
                out=a[:],
                in_=live[("w", j)][:],
                func=ACT.Exp,
                bias=live[("negmax", p)][:, i : i + 1],
                scale=1.0,
                accum_out=live[("rowsum", p)][:, i : i + 1],
            )
            live[("a", j)] = a

        def v4(p):
            rnorm = work.tile([P, 2], F32, tag="rnorm", bufs=4)
            nc.vector.reciprocal(out=rnorm[:], in_=live[("rowsum", p)][:])
            for i in range(2):
                attn = work.tile([P, H], BF16, tag="attn", bufs=4)
                nc.gpsimd.tensor_scalar(
                    out=attn[:],
                    in0=live[("a", 2 * p + i)][:],
                    scalar1=rnorm[:, i : i + 1],
                    scalar2=0.0,
                    op0=ALU.mult,
                    op1=ALU.add,
                )
                live[("attn", 2 * p + i)] = attn

        def t3(p):
            at = psum.tile([P, 2, 4, P], BF16, tag="at", bufs=1)
            for i in range(2):
                attn = live[("attn", 2 * p + i)]
                for t in range(4):
                    nc.tensor.transpose(at[:, i, t, :], attn[:, t * P : (t + 1) * P], ident_b[:])
            live[("at", p)] = at

        def x1(p):
            ga = work.tile([P, 2 * H], BF16, tag="ga", align_bytes=64)
            nc.vector.tensor_copy(
                out=ga[:].rearrange("q (i p t) -> q i p t", i=2, t=4),
                in_=live[("at", p)][:].rearrange("q i t p -> q i p t"),
            )
            live[("ga", p)] = ga

        def q2(p):
            aq = work.tile([P, 2 * P], U32, tag="aq", align_bytes=64)
            ac = work.tile([P, 2 * P], U8, tag="ac", align_bytes=64)
            nc.vector.quantize_mx(out=aq[:].bitcast(FP8X4), scales=ac[:], in_=live[("ga", p)][:])
            live[("aq", p)] = (aq, ac)

        def m2(j):
            b = j // TILES_PER_BATCH
            aq, ac = live[("aq", j // 2)]
            i = j % 2
            o = psum.tile([P, D], F32, tag="o", bufs=2)
            nc.tensor.matmul_mx(
                out=o[:],
                lhsT=aq[:, i * P : (i + 1) * P].bitcast(FP8X4),
                lhsT_scale=ac[:, i * P : (i + 1) * P],
                rhs=hq2[b][:].bitcast(FP8X4),
                rhs_scale=hc2[b][:],
                start=True,
                stop=True,
            )
            live[("o", j)] = o

        def x2(j, on_vector):
            p = j // 2
            i = j % 2
            if i == 0:
                osb = work.tile([P, 2 * D], F32, tag="osb", bufs=4)
                live[("osb", p)] = osb
            osb = live[("osb", p)]
            if on_vector:
                nc.vector.tensor_scalar(
                    out=osb[:, i * D : (i + 1) * D],
                    in0=live[("o", j)][:],
                    scalar1=pmf[:, j : j + 1],
                    scalar2=None,
                    op0=ALU.mult,
                )
            else:
                nc.scalar.activation(
                    out=osb[:, i * D : (i + 1) * D],
                    in_=live[("o", j)][:],
                    func=ACT.Copy,
                    scale=pmf[:, j : j + 1],
                )
            b = j // TILES_PER_BATCH
            c = j % TILES_PER_BATCH
            if p == NP - 1:
                nc.sync.dma_start(
                    out=out_view[b][:, c * D : (c + 1) * D], in_=osb[:, i * D : (i + 1) * D]
                )
            elif i == 1:
                nc.sync.dma_start(out=out_view[b][:, (c - 1) * D : (c + 1) * D], in_=osb[:])

        t1(("h1", 0), hs[0], 0, "o")
        t1(("h1", 0), hs[0], 1, "o")
        x3(("h1", 0), 0, True)
        x3(("h1", 0), 1, False)
        quantise(("h1", 0), hq1[0], hc1[0])

        def ok(p):
            return 0 <= p < NP

        def pa_on_vector(k):
            return k % 8 == 5

        def x2_on_vector(j):
            return j == NT - 1

        def x3_on_vector(p):
            return p >= 3

        for r in range(NP + 12):
            if ok(r - 1) and not x3_on_vector(r - 1):
                x3(("x", (r - 1) // 2), (r - 1) % 2, False)
            for i in range(2):
                if ok(r - 7):
                    pc(2 * (r - 7) + i)
                if ok(r - 11) and not x2_on_vector(2 * (r - 11) + i):
                    x2(2 * (r - 11) + i, False)
                if ok(r - 4) and not pa_on_vector(2 * (r - 4) + i):
                    pa(2 * (r - 4) + i, False)
            if ok(r - 4) and pa_on_vector(2 * (r - 4) + 1):
                pa(2 * (r - 4) + 1, True)
            if ok(r - 1) and x3_on_vector(r - 1):
                x3(("x", (r - 1) // 2), (r - 1) % 2, True)
            if r == 2 or r == 3:
                t1(("h1", 1), hs[1], r - 2, "o")
            if ok(r - 6):
                t2(2 * (r - 6))
            if ok(r - 9):
                t3(r - 9)
            if ok(r - 10):
                m2(2 * (r - 10))
            if ok(r - 6):
                t2(2 * (r - 6) + 1)
            if ok(r - 3):
                m1(2 * (r - 3))
            if ok(r - 10):
                m2(2 * (r - 10) + 1)
            if ok(r - 3):
                m1(2 * (r - 3) + 1)
            if ok(r):
                t1(("x", r // 2), xs[r // 2], r % 2, "pt")
            if r == 2 or r == 3:
                x3(("h1", 1), r - 2, False)
            if ok(r - 6):
                pb(2 * (r - 6))
            if ok(r - 9):
                x1(r - 9)
            if ok(r - 6):
                pb(2 * (r - 6) + 1)
            if r >= 2 and r % 2 == 0 and (r - 2) // 2 < NG:
                q1((r - 2) // 2)
            if r == 2:
                quantise(("h2", 0), hq2[0], hc2[0])
            if r == 4:
                quantise(("h2", 1), hq2[1], hc2[1])
            if r == 5:
                quantise(("h1", 1), hq1[1], hc1[1])
            if ok(r - 11) and x2_on_vector(2 * (r - 11) + 1):
                x2(2 * (r - 11) + 1, True)
            if r == 0:
                hyp_position_operand(0)
            if r == 2:
                hyp_mask_columns()
                hyp_position_operand(1)
            if r == 6:
                premise_mask_columns()
            if ok(r - 9):
                q2(r - 9)
            if ok(r - 7):
                v4(r - 7)
